import numpy as np
import ml_dtypes


def mxq(x, axis, fmt="e4m3"):
    dtype, down = {"e4m3": (ml_dtypes.float8_e4m3fn, 7), "e5m2": (ml_dtypes.float8_e5m2, 14)}[fmt]
    v = np.moveaxis(np.asarray(x, np.float32).astype(ml_dtypes.bfloat16).astype(np.float64), axis, -1)
    blocks = v.reshape(v.shape[:-1] + (-1, 32))
    amax = np.abs(blocks).max(-1, keepdims=True)
    byte = np.maximum(np.where(amax > 0, np.frexp(amax)[1] - 1 + 127, 0) - down, 1)
    scale = np.exp2(byte - 127.0)
    codes = (blocks / scale).astype(np.float32).astype(dtype).astype(np.float64)
    return np.moveaxis((codes * scale).reshape(v.shape), -1, axis)


WIDE = False


def mx_kscale(k):
    if not WIDE:
        return np.ones(k)
    levels = np.array([10, -10, 5, -5, 0])
    a = np.random.permutation(np.resize(levels, k // 512 * 4)).reshape(k // 512, 4)
    idx = np.arange(k)
    return np.exp2(a[idx // 512, idx % 128 // 32])


BF16 = ml_dtypes.bfloat16


def bf(x):
    return np.asarray(x, np.float32).astype(BF16)


def f64(x):
    return np.asarray(x).astype(np.float64)


B, F_IN, HID, E, G, H = 4096, 64, 1024, 32, 4, 8
BN_EPS = 1e-5
L1_EPS = 1e-6 ** 2
SELU_ALPHA = 1.6732632423543772
SELU_SCALE = 1.0507009873554805


def selu(v):
    return SELU_SCALE * np.where(v > 0.0, v, SELU_ALPHA * (np.exp(np.minimum(v, 0.0)) - 1.0))


def setup_inputs():
    s = mx_kscale(HID)
    t = s / s.min()
    col_std = 0.5 + np.random.random(HID)
    col_mean = 0.5 * np.random.standard_normal(HID)
    return {"h2": bf(np.random.standard_normal((B, HID)) * col_std + col_mean),
            "gamma": bf((1.0 + 0.1 * np.random.standard_normal(HID)) * t),
            "beta": bf(0.1 * np.random.standard_normal(HID) * t),
            "Wh": bf(np.random.standard_normal((H, G, HID, E)) / np.sqrt(HID) / t[:, None]),
            "bh": bf(0.3 * np.random.standard_normal((H, G, E)))}


def reference(h2, gamma, beta, Wh, bh):
    h2 = f64(h2)
    mu = h2.mean(axis=0)
    var = h2.var(axis=0)
    e = selu((h2 - mu) / np.sqrt(var + BN_EPS) * f64(gamma) + f64(beta))
    p = (mxq(e, 1, "e4m3") @ mxq(f64(Wh), 2, "e4m3")).transpose(2, 0, 1, 3)
    d = selu(p + f64(bh))
    a = np.abs(d)
    l1 = np.maximum(a.sum(axis=-1, keepdims=True), L1_EPS)
    return np.sign(d) * (a / l1)

@@ -1,0 +1,254 @@
+import math
+
+import concourse.bass as bass
+import concourse.mybir as mybir
+import concourse.tile as tile
+from concourse.masks import make_identity
+
+F32 = mybir.dt.float32
+BF16 = mybir.dt.bfloat16
+U32 = mybir.dt.uint32
+U8 = mybir.dt.uint8
+FP8X4 = mybir.dt.float8_e4m3fn_x4
+ALU = mybir.AluOpType
+ACT = mybir.ActivationFunctionType
+AXIS = mybir.AxisListType
+
+P = 128
+ROWS = 4096
+HID = 1024
+OUTS = 1024
+HEAD = 32
+ROW_TILES = ROWS // P
+WORD_BLOCKS = HID // 2 // P
+PLANES = 2 * WORD_BLOCKS
+PASSES = HID // 512
+
+LOAD_TILES = 4
+LOAD_COLS = LOAD_TILES * P
+STAT_COLS = 256
+UNIT = 512
+
+BN_EPS = 1e-5
+L1_EPS = 1e-12
+SELU_ALPHA = 1.6732632423543772
+SELU_SCALE = 1.0507009873554805
+SA = SELU_SCALE * SELU_ALPHA
+
+FLOPS = 2 * ROWS * HID * OUTS
+
+
+def tile_basicemotionpredictions_pa_t_kernel(tc, h2, gamma, beta, Wh, bh, out):
+    nc = tc.nc
+    h2_v = h2.rearrange("(p n) f -> p n f", n=ROW_TILES)
+    out_v = out.rearrange("(p n) h g e -> p n (h g e)", n=ROW_TILES)
+    wh_v = Wh.rearrange("h g (cu q e2) e -> q (h g cu) (e2 e)", cu=WORD_BLOCKS, q=P, e2=2)
+
+    with tc.tile_pool(name="keep", bufs=1) as keep, tc.tile_pool(name="stream", bufs=3) as stream, tc.tile_pool(
+        name="qin", bufs=2
+    ) as qin, tc.tile_pool(name="work", bufs=2) as work, tc.tile_pool(name="codes", bufs=3) as codes, tc.tile_pool(
+        name="post", bufs=2
+    ) as post, tc.tile_pool(name="small", bufs=3) as small, tc.psum_pool(name="psum_mm", bufs=4) as psum_mm, tc.psum_pool(
+        name="psum_tr", bufs=4
+    ) as psum_tr:
+        warm = keep.tile([P, 1], F32)
+        nc.vector.memset(warm[:], 1.0)
+        warm_out = keep.tile([P, 1], F32)
+        nc.scalar.activation(out=warm_out[:], in_=warm[:], func=ACT.Sqrt)
+        zero = keep.tile([P, 1], F32)
+        nc.vector.memset(zero[:], 0.0)
+        ln_sa = keep.tile([P, 1], F32)
+        nc.vector.tensor_scalar_add(out=ln_sa[:], in0=zero[:], scalar1=math.log(SA))
+
+        ident = keep.tile([P, P], F32)
+        make_identity(nc, ident[:])
+
+        gamma_sb = keep.tile([P, WORD_BLOCKS, 2], BF16)
+        beta_sb = keep.tile([P, WORD_BLOCKS, 2], BF16)
+        bh_sb = keep.tile([P, OUTS // P], BF16)
+        nc.scalar.dma_start(out=gamma_sb[:], in_=gamma.rearrange("(wb q e2) -> q wb e2", wb=WORD_BLOCKS, q=P))
+        nc.scalar.dma_start(out=beta_sb[:], in_=beta.rearrange("(wb q e2) -> q wb e2", wb=WORD_BLOCKS, q=P))
+        with nc.allow_non_contiguous_dma(reason="1,024 bias values, one output to a partition"):
+            nc.scalar.dma_start(out=bh_sb[:], in_=bh.rearrange("h g e -> (h g e)").rearrange("(ob o) -> o ob", o=P))
+
+        bias_rel = keep.tile([P, OUTS // P], F32)
+        bias_exp = keep.tile([P, OUTS // P], F32)
+        nc.vector.tensor_copy(out=bias_rel[:], in_=bh_sb[:])
+        nc.vector.tensor_scalar_add(out=bias_exp[:], in0=bias_rel[:], scalar1=math.log(SELU_ALPHA))
+
+        x_t = keep.tile([P, WORD_BLOCKS, ROWS], F32)
+        stats = keep.tile([P, WORD_BLOCKS, ROWS // STAT_COLS, 6], F32)
+        for ld in range(ROW_TILES // LOAD_TILES):
+            x_sb = stream.tile([P, LOAD_TILES, HID], BF16, tag="stream")
+            nc.sync.dma_start(out=x_sb[:], in_=h2_v[:, LOAD_TILES * ld : LOAD_TILES * (ld + 1), :])
+            for wb in range(WORD_BLOCKS):
+                xt_ps = psum_tr.tile([P, LOAD_COLS], F32, tag="tr")
+                for i in range(LOAD_TILES):
+                    nc.tensor.transpose(
+                        xt_ps[:, P * i : P * (i + 1)],
+                        x_sb[:, i, :].bitcast(F32)[:, P * wb : P * (wb + 1)],
+                        ident[:],
+                    )
+                nc.scalar.copy(out=x_t[:, wb, LOAD_COLS * ld : LOAD_COLS * (ld + 1)], in_=xt_ps[:])
+                for s in range(LOAD_COLS // STAT_COLS):
+                    first = LOAD_COLS * ld + STAT_COLS * s
+                    nc.vector.bn_stats(
+                        out=stats[:, wb, first // STAT_COLS, :],
+                        in_=x_t[:, wb, first : first + STAT_COLS].bitcast(BF16),
+                    )
+
+        w_raws = []
+        for hf in range(2):
+            w_raw = stream.tile([P, 16, PLANES, HEAD], BF16, tag="stream")
+            nc.sync.dma_start(
+                out=w_raw[:].rearrange("q hg (cu e2) e -> q (hg cu) (e2 e)", e2=2),
+                in_=wh_v[:, 64 * hf : 64 * (hf + 1), :],
+            )
+            w_raws.append(w_raw)
+
+        mv = keep.tile([P, PLANES, 2], F32)
+        for wb in range(WORD_BLOCKS):
+            for e2 in range(2):
+                nc.vector.bn_aggr(out=mv[:, 2 * wb + e2, :], in_=stats[:, wb, :, 3 * e2 : 3 * e2 + 3])
+        var_eps = keep.tile([P, PLANES], F32)
+        std = keep.tile([P, PLANES], F32)
+        rstd = keep.tile([P, PLANES], F32)
+        a_lin = keep.tile([P, PLANES], F32)
+        a_neg = keep.tile([P, PLANES], F32)
+        b_neg = keep.tile([P, PLANES], F32)
+        a_rel = keep.tile([P, PLANES], F32)
+        b_rel = keep.tile([P, PLANES], F32)
+        nc.vector.tensor_scalar_add(out=var_eps[:], in0=mv[:, :, 1], scalar1=BN_EPS)
+        nc.scalar.activation(out=std[:], in_=var_eps[:], func=ACT.Sqrt)
+        nc.vector.reciprocal(out=rstd[:], in_=std[:])
+        nc.vector.tensor_tensor(out=a_lin[:], in0=gamma_sb[:].rearrange("q wb e2 -> q (wb e2)"), in1=rstd[:], op=ALU.mult)
+        nc.vector.tensor_tensor(out=b_neg[:], in0=mv[:, :, 0], in1=a_lin[:], op=ALU.mult)
+        nc.vector.tensor_tensor(out=b_neg[:], in0=b_neg[:], in1=beta_sb[:].rearrange("q wb e2 -> q (wb e2)"), op=ALU.subtract)
+        nc.vector.tensor_scalar_mul(out=a_neg[:], in0=a_lin[:], scalar1=-1.0)
+        nc.vector.tensor_scalar_mul(out=a_rel[:], in0=a_lin[:], scalar1=SELU_SCALE)
+        neg_e0 = keep.tile([P, 1], F32)
+        nc.scalar.activation(out=neg_e0[:], in_=zero[:], func=ACT.Exp, bias=ln_sa[:])
+        nc.vector.tensor_scalar_mul(out=neg_e0[:], in0=neg_e0[:], scalar1=-1.0)
+        nc.vector.tensor_scalar(
+            out=b_rel[:], in0=b_neg[:], scalar1=-SELU_SCALE, scalar2=neg_e0[:], op0=ALU.mult, op1=ALU.add
+        )
+
+        w_codes = keep.tile([P, 2, PASSES, 512], U32, align_bytes=64)
+        w_scales = keep.tile([P, 2, PASSES, 512], U8, align_bytes=64)
+        for hf in range(2):
+            for c in range(PASSES):
+                w_grouped = qin.tile([P, 512, 4], BF16, tag="grouped", align_bytes=64)
+                nc.vector.tensor_copy(
+                    out=w_grouped[:].rearrange("q (hg e) t -> q hg e t", e=HEAD),
+                    in_=w_raws[hf][:, :, 4 * c : 4 * (c + 1), :].rearrange("q hg t e -> q hg e t"),
+                )
+                nc.vector.quantize_mx(
+                    out=w_codes[:, hf, c, :].bitcast(FP8X4),
+                    scales=w_scales[:, hf, c, :],
+                    in_=w_grouped[:].rearrange("q o t -> q (o t)"),
+                )
+
+        def quantise_pass(u, c, e_codes, e_scales):
+            e_exp = work.tile([P, 4, UNIT], F32)
+            e_lin = work.tile([P, 4, UNIT], F32)
+            for t in range(4):
+                wb = 2 * c + t // 2
+                plane = 4 * c + t
+                x_plane = (
+                    x_t[:, wb, UNIT * u : UNIT * (u + 1)]
+                    .bitcast(BF16)
+                    .rearrange("q (j e2) -> q j e2", e2=2)[:, :, t % 2]
+                )
+                nc.scalar.activation(
+                    out=e_exp[:, t, :], in_=x_plane, func=ACT.Relu,
+                    scale=a_neg[:, plane : plane + 1], bias=b_neg[:, plane : plane + 1],
+                )
+                nc.gpsimd.tensor_scalar(
+                    out=e_lin[:, t, :], in0=x_plane,
+                    scalar1=a_rel[:, plane : plane + 1], scalar2=b_rel[:, plane : plane + 1],
+                    op0=ALU.mult, op1=ALU.add,
+                )
+            nc.scalar.activation(out=e_exp[:], in_=e_exp[:], func=ACT.Exp, scale=-1.0, bias=ln_sa[:])
+            e_grouped = qin.tile([P, UNIT, 4], BF16, tag="grouped", align_bytes=64)
+            nc.vector.scalar_tensor_tensor(
+                out=e_grouped[:],
+                in0=e_lin[:].rearrange("q t j -> q j t"),
+                scalar=neg_e0[:],
+                in1=e_exp[:].rearrange("q t j -> q j t"),
+                op0=ALU.max,
+                op1=ALU.add,
+            )
+            nc.vector.quantize_mx(
+                out=e_codes[:, c, :].bitcast(FP8X4),
+                scales=e_scales[:, c, :],
+                in_=e_grouped[:].rearrange("q j t -> q (j t)"),
+            )
+
+        def heads(u, hf, e_codes, e_scales):
+            z_exp = post.tile([P, 4, UNIT], F32, bufs=3)
+            z_rel = post.tile([P, 4, UNIT], F32)
+            for ob4 in range(4):
+                ob = 4 * hf + ob4
+                w_cols = slice(P * ob4, P * (ob4 + 1))
+                acc = psum_mm.tile([P, UNIT], F32)
+                for c in range(PASSES):
+                    nc.tensor.matmul_mx(
+                        out=acc[:],
+                        lhsT=w_codes[:, hf, c, w_cols].bitcast(FP8X4),
+                        lhsT_scale=w_scales[:, hf, c, w_cols],
+                        rhs=e_codes[:, c, :].bitcast(FP8X4),
+                        rhs_scale=e_scales[:, c, :],
+                        start=(c == 0),
+                        stop=(c == PASSES - 1),
+                    )
+                nc.scalar.activation(out=z_exp[:, ob4, :], in_=acc[:], func=ACT.Exp, bias=bias_exp[:, ob : ob + 1])
+                nc.scalar.activation(out=z_rel[:, ob4, :], in_=acc[:], func=ACT.Relu, bias=bias_rel[:, ob : ob + 1])
+            nc.vector.scalar_tensor_tensor(
+                out=z_exp[:], in0=z_exp[:], scalar=-SELU_ALPHA, in1=z_rel[:], op0=ALU.add, op1=ALU.min
+            )
+            l1 = small.tile([P, 4, 512 // HEAD], F32)
+            r_l1 = small.tile([P, 4, 512 // HEAD], F32)
+            d_abs = post.tile([P, 4, 512], F32)
+            d_ts = []
+            for nt in range(4):
+                d_t = psum_tr.tile([P, 512], F32, tag="tr")
+                for ob4 in range(4):
+                    nc.tensor.transpose(
+                        d_t[:, P * ob4 : P * (ob4 + 1)], z_exp[:, ob4, P * nt : P * (nt + 1)], ident[:]
+                    )
+                nc.scalar.activation(out=d_abs[:, nt, :], in_=d_t[:], func=ACT.Abs)
+                d_ts.append(d_t)
+            nc.vector.tensor_reduce(
+                out=l1[:].rearrange("p nt g -> p (nt g)"),
+                in_=d_abs[:].rearrange("p nt (g e) -> p (nt g) e", e=HEAD),
+                axis=AXIS.X,
+                op=ALU.add,
+            )
+            nc.vector.tensor_scalar_max(out=l1[:], in0=l1[:], scalar1=L1_EPS / SELU_SCALE)
+            nc.vector.reciprocal(out=r_l1[:], in_=l1[:])
+            out_sb = stream.tile([P, 4, 512], F32, tag="stream")
+            for nt in range(4):
+                nc.vector.tensor_tensor(
+                    out=out_sb[:, nt, :].rearrange("p (g e) -> p g e", e=HEAD),
+                    in0=d_ts[nt][:].rearrange("p (g e) -> p g e", e=HEAD),
+                    in1=r_l1[:, nt, :].unsqueeze(2).to_broadcast([P, 512 // HEAD, HEAD]),
+                    op=ALU.mult,
+                )
+            first_tile = UNIT * u // P
+            nc.sync.dma_start(out=out_v[:, first_tile : first_tile + 4, 512 * hf : 512 * (hf + 1)], in_=out_sb[:])
+
+        def quantise_unit(u):
+            e_codes = codes.tile([P, PASSES, UNIT], U32, align_bytes=64)
+            e_scales = codes.tile([P, PASSES, UNIT], U8, align_bytes=64)
+            for c in range(PASSES):
+                quantise_pass(u, c, e_codes, e_scales)
+            return e_codes, e_scales
+
+        units = ROWS // UNIT
+        ahead = quantise_unit(0)
+        for u in range(units):
+            now = ahead
+            if u + 1 < units:
+                ahead = quantise_unit(u + 1)
+            for hf in range(2):
+                heads(u, hf, now[0], now[1])

@@ -46,7 +46,7 @@ def tile_basicemotionpredictions_pa_t_kernel(tc, h2, gamma, beta, Wh, bh, out):
 
     with tc.tile_pool(name="keep", bufs=1) as keep, tc.tile_pool(name="stream", bufs=3) as stream, tc.tile_pool(
         name="qin", bufs=2
-    ) as qin, tc.tile_pool(name="work", bufs=2) as work, tc.tile_pool(name="codes", bufs=3) as codes, tc.tile_pool(
+    ) as qin, tc.tile_pool(name="work", bufs=3) as work, tc.tile_pool(name="codes", bufs=3) as codes, tc.tile_pool(
         name="post", bufs=2
     ) as post, tc.tile_pool(name="small", bufs=3) as small, tc.psum_pool(name="psum_mm", bufs=4) as psum_mm, tc.psum_pool(
         name="psum_tr", bufs=4
@@ -57,8 +57,10 @@ def tile_basicemotionpredictions_pa_t_kernel(tc, h2, gamma, beta, Wh, bh, out):
         nc.scalar.activation(out=warm_out[:], in_=warm[:], func=ACT.Sqrt)
         zero = keep.tile([P, 1], F32)
         nc.vector.memset(zero[:], 0.0)
-        ln_sa = keep.tile([P, 1], F32)
-        nc.vector.tensor_scalar_add(out=ln_sa[:], in0=zero[:], scalar1=math.log(SA))
+        minus_sa = keep.tile([P, 1], F32)
+        nc.vector.tensor_scalar_add(out=minus_sa[:], in0=zero[:], scalar1=-SA)
+        exp_bias = keep.tile([P, 1], F32)
+        nc.vector.tensor_scalar_add(out=exp_bias[:], in0=zero[:], scalar1=SELU_ALPHA + math.log(SA))
 
         ident = keep.tile([P, P], F32)
         make_identity(nc, ident[:])
@@ -114,7 +116,6 @@ def tile_basicemotionpredictions_pa_t_kernel(tc, h2, gamma, beta, Wh, bh, out):
         std = keep.tile([P, PLANES], F32)
         rstd = keep.tile([P, PLANES], F32)
         a_lin = keep.tile([P, PLANES], F32)
-        a_neg = keep.tile([P, PLANES], F32)
         b_neg = keep.tile([P, PLANES], F32)
         a_rel = keep.tile([P, PLANES], F32)
         b_rel = keep.tile([P, PLANES], F32)
@@ -124,10 +125,9 @@ def tile_basicemotionpredictions_pa_t_kernel(tc, h2, gamma, beta, Wh, bh, out):
         nc.vector.tensor_tensor(out=a_lin[:], in0=gamma_sb[:].rearrange("q wb e2 -> q (wb e2)"), in1=rstd[:], op=ALU.mult)
         nc.vector.tensor_tensor(out=b_neg[:], in0=mv[:, :, 0], in1=a_lin[:], op=ALU.mult)
         nc.vector.tensor_tensor(out=b_neg[:], in0=b_neg[:], in1=beta_sb[:].rearrange("q wb e2 -> q (wb e2)"), op=ALU.subtract)
-        nc.vector.tensor_scalar_mul(out=a_neg[:], in0=a_lin[:], scalar1=-1.0)
         nc.vector.tensor_scalar_mul(out=a_rel[:], in0=a_lin[:], scalar1=SELU_SCALE)
         neg_e0 = keep.tile([P, 1], F32)
-        nc.scalar.activation(out=neg_e0[:], in_=zero[:], func=ACT.Exp, bias=ln_sa[:])
+        nc.scalar.activation(out=neg_e0[:], in_=minus_sa[:], func=ACT.Exp, scale=1.0 / SELU_SCALE, bias=exp_bias[:])
         nc.vector.tensor_scalar_mul(out=neg_e0[:], in0=neg_e0[:], scalar1=-1.0)
         nc.vector.tensor_scalar(
             out=b_rel[:], in0=b_neg[:], scalar1=-SELU_SCALE, scalar2=neg_e0[:], op0=ALU.mult, op1=ALU.add
@@ -148,7 +148,17 @@ def tile_basicemotionpredictions_pa_t_kernel(tc, h2, gamma, beta, Wh, bh, out):
                     in_=w_grouped[:].rearrange("q o t -> q (o t)"),
                 )
 
-        def quantise_pass(u, c, e_codes, e_scales):
+        steps = 2 * (ROWS // UNIT)
+        branch_tiles = {}
+        code_tiles = {}
+        acc_tiles = {}
+        z_tiles = {}
+        d_t_tiles = {}
+        abs_tiles = {}
+
+        def linear_branch(q):
+            u = q // 2
+            c = q % 2
             e_exp = work.tile([P, 4, UNIT], F32)
             e_lin = work.tile([P, 4, UNIT], F32)
             for t in range(4):
@@ -159,16 +169,29 @@ def tile_basicemotionpredictions_pa_t_kernel(tc, h2, gamma, beta, Wh, bh, out):
                     .bitcast(BF16)
                     .rearrange("q (j e2) -> q j e2", e2=2)[:, :, t % 2]
                 )
-                nc.scalar.activation(
-                    out=e_exp[:, t, :], in_=x_plane, func=ACT.Relu,
-                    scale=a_neg[:, plane : plane + 1], bias=b_neg[:, plane : plane + 1],
-                )
                 nc.gpsimd.tensor_scalar(
                     out=e_lin[:, t, :], in0=x_plane,
                     scalar1=a_rel[:, plane : plane + 1], scalar2=b_rel[:, plane : plane + 1],
                     op0=ALU.mult, op1=ALU.add,
                 )
-            nc.scalar.activation(out=e_exp[:], in_=e_exp[:], func=ACT.Exp, scale=-1.0, bias=ln_sa[:])
+            nc.gpsimd.tensor_scalar(
+                out=e_exp[:], in0=e_lin[:], scalar1=-SA, scalar2=-3.0e38, op0=ALU.min, op1=ALU.max
+            )
+            branch_tiles[q] = (e_exp, e_lin)
+
+        def exp_branch(q):
+            e_exp = branch_tiles[q][0]
+            nc.scalar.activation(out=e_exp[:], in_=e_exp[:], func=ACT.Exp, scale=1.0 / SELU_SCALE, bias=exp_bias[:])
+
+        def join_and_quantise(q):
+            u = q // 2
+            c = q % 2
+            if c == 0:
+                e_codes = codes.tile([P, PASSES, UNIT], U32, align_bytes=64)
+                e_scales = codes.tile([P, PASSES, UNIT], U8, align_bytes=64)
+                code_tiles[u] = (e_codes, e_scales)
+            e_codes, e_scales = code_tiles[u]
+            e_exp, e_lin = branch_tiles[q]
             e_grouped = qin.tile([P, UNIT, 4], BF16, tag="grouped", align_bytes=64)
             nc.vector.scalar_tensor_tensor(
                 out=e_grouped[:],
@@ -184,11 +207,11 @@ def tile_basicemotionpredictions_pa_t_kernel(tc, h2, gamma, beta, Wh, bh, out):
                 in_=e_grouped[:].rearrange("q j t -> q (j t)"),
             )
 
-        def heads(u, hf, e_codes, e_scales):
-            z_exp = post.tile([P, 4, UNIT], F32, bufs=3)
-            z_rel = post.tile([P, 4, UNIT], F32)
+        def products(i):
+            hf = i % 2
+            e_codes, e_scales = code_tiles[i // 2]
+            accs = []
             for ob4 in range(4):
-                ob = 4 * hf + ob4
                 w_cols = slice(P * ob4, P * (ob4 + 1))
                 acc = psum_mm.tile([P, UNIT], F32)
                 for c in range(PASSES):
@@ -201,26 +224,47 @@ def tile_basicemotionpredictions_pa_t_kernel(tc, h2, gamma, beta, Wh, bh, out):
                         start=(c == 0),
                         stop=(c == PASSES - 1),
                     )
+                accs.append(acc)
+            acc_tiles[i] = accs
+
+        def head_branches(i):
+            z_exp = post.tile([P, 4, UNIT], F32)
+            z_rel = post.tile([P, 4, UNIT], F32)
+            for ob4 in range(4):
+                ob = 4 * (i % 2) + ob4
+                acc = acc_tiles[i][ob4]
                 nc.scalar.activation(out=z_exp[:, ob4, :], in_=acc[:], func=ACT.Exp, bias=bias_exp[:, ob : ob + 1])
                 nc.scalar.activation(out=z_rel[:, ob4, :], in_=acc[:], func=ACT.Relu, bias=bias_rel[:, ob : ob + 1])
+            z_tiles[i] = (z_exp, z_rel)
+
+        def head_selu(i):
+            z_exp, z_rel = z_tiles[i]
             nc.vector.scalar_tensor_tensor(
                 out=z_exp[:], in0=z_exp[:], scalar=-SELU_ALPHA, in1=z_rel[:], op0=ALU.add, op1=ALU.min
             )
-            l1 = small.tile([P, 4, 512 // HEAD], F32)
-            r_l1 = small.tile([P, 4, 512 // HEAD], F32)
-            d_abs = post.tile([P, 4, 512], F32)
+
+        def transpose_back(i):
+            z_exp = z_tiles[i][0]
             d_ts = []
             for nt in range(4):
                 d_t = psum_tr.tile([P, 512], F32, tag="tr")
                 for ob4 in range(4):
-                    nc.tensor.transpose(
-                        d_t[:, P * ob4 : P * (ob4 + 1)], z_exp[:, ob4, P * nt : P * (nt + 1)], ident[:]
-                    )
-                nc.scalar.activation(out=d_abs[:, nt, :], in_=d_t[:], func=ACT.Abs)
+                    nc.tensor.transpose(d_t[:, P * ob4 : P * (ob4 + 1)], z_exp[:, ob4, P * nt : P * (nt + 1)], ident[:])
                 d_ts.append(d_t)
+            d_t_tiles[i] = d_ts
+
+        def magnitudes(i):
+            d_abs = post.tile([P, 4, 512], F32)
+            for nt in range(4):
+                nc.scalar.activation(out=d_abs[:, nt, :], in_=d_t_tiles[i][nt][:], func=ACT.Abs)
+            abs_tiles[i] = d_abs
+
+        def normalise_and_store(i):
+            l1 = small.tile([P, 4, 512 // HEAD], F32)
+            r_l1 = small.tile([P, 4, 512 // HEAD], F32)
             nc.vector.tensor_reduce(
                 out=l1[:].rearrange("p nt g -> p (nt g)"),
-                in_=d_abs[:].rearrange("p nt (g e) -> p (nt g) e", e=HEAD),
+                in_=abs_tiles[i][:].rearrange("p nt (g e) -> p (nt g) e", e=HEAD),
                 axis=AXIS.X,
                 op=ALU.add,
             )
@@ -230,25 +274,31 @@ def tile_basicemotionpredictions_pa_t_kernel(tc, h2, gamma, beta, Wh, bh, out):
             for nt in range(4):
                 nc.vector.tensor_tensor(
                     out=out_sb[:, nt, :].rearrange("p (g e) -> p g e", e=HEAD),
-                    in0=d_ts[nt][:].rearrange("p (g e) -> p g e", e=HEAD),
+                    in0=d_t_tiles[i][nt][:].rearrange("p (g e) -> p g e", e=HEAD),
                     in1=r_l1[:, nt, :].unsqueeze(2).to_broadcast([P, 512 // HEAD, HEAD]),
                     op=ALU.mult,
                 )
-            first_tile = UNIT * u // P
+            first_tile = UNIT * (i // 2) // P
+            hf = i % 2
             nc.sync.dma_start(out=out_v[:, first_tile : first_tile + 4, 512 * hf : 512 * (hf + 1)], in_=out_sb[:])
 
-        def quantise_unit(u):
-            e_codes = codes.tile([P, PASSES, UNIT], U32, align_bytes=64)
-            e_scales = codes.tile([P, PASSES, UNIT], U8, align_bytes=64)
-            for c in range(PASSES):
-                quantise_pass(u, c, e_codes, e_scales)
-            return e_codes, e_scales
-
-        units = ROWS // UNIT
-        ahead = quantise_unit(0)
-        for u in range(units):
-            now = ahead
-            if u + 1 < units:
-                ahead = quantise_unit(u + 1)
-            for hf in range(2):
-                heads(u, hf, now[0], now[1])
+        with tc.manual_schedule():
+            for i in range(-4, steps + 1):
+                if 0 <= i < steps:
+                    head_branches(i)
+                if 0 <= i - 1 < steps:
+                    magnitudes(i - 1)
+                if 0 <= i + 4 < steps:
+                    linear_branch(i + 4)
+                if 0 <= i + 3 < steps:
+                    exp_branch(i + 3)
+                if 0 <= i + 2 < steps:
+                    join_and_quantise(i + 2)
+                if 0 <= i + 1 < steps:
+                    products(i + 1)
+                if 0 <= i < steps:
+                    head_selu(i)
+                if 0 <= i - 1 < steps:
+                    normalise_and_store(i - 1)
+                if 0 <= i < steps:
+                    transpose_back(i)

@@ -46,7 +46,7 @@ def tile_basicemotionpredictions_pa_t_kernel(tc, h2, gamma, beta, Wh, bh, out):
 
     with tc.tile_pool(name="keep", bufs=1) as keep, tc.tile_pool(name="stream", bufs=3) as stream, tc.tile_pool(
         name="qin", bufs=2
-    ) as qin, tc.tile_pool(name="work", bufs=3) as work, tc.tile_pool(name="codes", bufs=3) as codes, tc.tile_pool(
+    ) as qin, tc.tile_pool(name="work", bufs=3) as work, tc.tile_pool(name="codes", bufs=4) as codes, tc.tile_pool(
         name="post", bufs=2
     ) as post, tc.tile_pool(name="small", bufs=3) as small, tc.psum_pool(name="psum_mm", bufs=4) as psum_mm, tc.psum_pool(
         name="psum_tr", bufs=4
@@ -61,6 +61,8 @@ def tile_basicemotionpredictions_pa_t_kernel(tc, h2, gamma, beta, Wh, bh, out):
         nc.vector.tensor_scalar_add(out=minus_sa[:], in0=zero[:], scalar1=-SA)
         exp_bias = keep.tile([P, 1], F32)
         nc.vector.tensor_scalar_add(out=exp_bias[:], in0=zero[:], scalar1=SELU_ALPHA + math.log(SA))
+        ln_sa = keep.tile([P, 1], F32)
+        nc.vector.tensor_scalar_add(out=ln_sa[:], in0=zero[:], scalar1=math.log(SA))
 
         ident = keep.tile([P, P], F32)
         make_identity(nc, ident[:])
@@ -126,41 +128,46 @@ def tile_basicemotionpredictions_pa_t_kernel(tc, h2, gamma, beta, Wh, bh, out):
         nc.vector.tensor_tensor(out=b_neg[:], in0=mv[:, :, 0], in1=a_lin[:], op=ALU.mult)
         nc.vector.tensor_tensor(out=b_neg[:], in0=b_neg[:], in1=beta_sb[:].rearrange("q wb e2 -> q (wb e2)"), op=ALU.subtract)
         nc.vector.tensor_scalar_mul(out=a_rel[:], in0=a_lin[:], scalar1=SELU_SCALE)
-        neg_e0 = keep.tile([P, 1], F32)
-        nc.scalar.activation(out=neg_e0[:], in_=minus_sa[:], func=ACT.Exp, scale=1.0 / SELU_SCALE, bias=exp_bias[:])
+        neg_e0 = keep.tile([P, PASSES], F32)
+        nc.scalar.activation(out=neg_e0[:, 0:1], in_=zero[:], func=ACT.Exp, scale=-1.0 / SELU_SCALE, bias=ln_sa[:])
+        nc.scalar.activation(out=neg_e0[:, 1:2], in_=minus_sa[:], func=ACT.Exp, scale=1.0 / SELU_SCALE, bias=exp_bias[:])
         nc.vector.tensor_scalar_mul(out=neg_e0[:], in0=neg_e0[:], scalar1=-1.0)
-        nc.vector.tensor_scalar(
-            out=b_rel[:], in0=b_neg[:], scalar1=-SELU_SCALE, scalar2=neg_e0[:], op0=ALU.mult, op1=ALU.add
-        )
+        for c in range(PASSES):
+            nc.vector.tensor_scalar(
+                out=b_rel[:, 4 * c : 4 * (c + 1)], in0=b_neg[:, 4 * c : 4 * (c + 1)],
+                scalar1=-SELU_SCALE, scalar2=neg_e0[:, c : c + 1], op0=ALU.mult, op1=ALU.add,
+            )
 
         w_codes = keep.tile([P, 2, PASSES, 512], U32, align_bytes=64)
         w_scales = keep.tile([P, 2, PASSES, 512], U8, align_bytes=64)
-        for hf in range(2):
-            for c in range(PASSES):
-                w_grouped = qin.tile([P, 512, 4], BF16, tag="grouped", align_bytes=64)
-                nc.vector.tensor_copy(
-                    out=w_grouped[:].rearrange("q (hg e) t -> q hg e t", e=HEAD),
-                    in_=w_raws[hf][:, :, 4 * c : 4 * (c + 1), :].rearrange("q hg t e -> q hg e t"),
-                )
-                nc.vector.quantize_mx(
-                    out=w_codes[:, hf, c, :].bitcast(FP8X4),
-                    scales=w_scales[:, hf, c, :],
-                    in_=w_grouped[:].rearrange("q o t -> q (o t)"),
-                )
+
+        def quantise_weights(hf, c):
+            w_grouped = qin.tile([P, 512, 4], BF16, tag="grouped", align_bytes=64)
+            nc.vector.tensor_copy(
+                out=w_grouped[:].rearrange("q (hg e) t -> q hg e t", e=HEAD),
+                in_=w_raws[hf][:, :, 4 * c : 4 * (c + 1), :].rearrange("q hg t e -> q hg e t"),
+            )
+            nc.vector.quantize_mx(
+                out=w_codes[:, hf, c, :].bitcast(FP8X4),
+                scales=w_scales[:, hf, c, :],
+                in_=w_grouped[:].rearrange("q o t -> q (o t)"),
+            )
 
         steps = 2 * (ROWS // UNIT)
-        branch_tiles = {}
+        lin_tiles = {}
+        exp_tiles = {}
+        grouped_tiles = {}
         code_tiles = {}
         acc_tiles = {}
         z_tiles = {}
         d_t_tiles = {}
         abs_tiles = {}
+        l1_tiles = {}
 
         def linear_branch(q):
             u = q // 2
             c = q % 2
-            e_exp = work.tile([P, 4, UNIT], F32)
-            e_lin = work.tile([P, 4, UNIT], F32)
+            e_lin = work.tile([P, 4, UNIT], F32, bufs=3)
             for t in range(4):
                 wb = 2 * c + t // 2
                 plane = 4 * c + t
@@ -174,16 +181,31 @@ def tile_basicemotionpredictions_pa_t_kernel(tc, h2, gamma, beta, Wh, bh, out):
                     scalar1=a_rel[:, plane : plane + 1], scalar2=b_rel[:, plane : plane + 1],
                     op0=ALU.mult, op1=ALU.add,
                 )
-            nc.gpsimd.tensor_scalar(
-                out=e_exp[:], in0=e_lin[:], scalar1=-SA, scalar2=-3.0e38, op0=ALU.min, op1=ALU.max
-            )
-            branch_tiles[q] = (e_exp, e_lin)
+            lin_tiles[q] = e_lin
 
         def exp_branch(q):
-            e_exp = branch_tiles[q][0]
-            nc.scalar.activation(out=e_exp[:], in_=e_exp[:], func=ACT.Exp, scale=1.0 / SELU_SCALE, bias=exp_bias[:])
+            e_exp = work.tile([P, 4, UNIT], F32, bufs=2)
+            if q % 2 == 0:
+                nc.scalar.activation(out=e_exp[:], in_=lin_tiles[q][:], func=ACT.Relu, scale=-1.0, bias=minus_sa[:])
+                nc.scalar.activation(out=e_exp[:], in_=e_exp[:], func=ACT.Exp, scale=-1.0 / SELU_SCALE, bias=ln_sa[:])
+            else:
+                nc.vector.tensor_scalar_min(out=e_exp[:], in0=lin_tiles[q][:], scalar1=-SA)
+                nc.scalar.activation(out=e_exp[:], in_=e_exp[:], func=ACT.Exp, scale=1.0 / SELU_SCALE, bias=exp_bias[:])
+            exp_tiles[q] = e_exp
 
-        def join_and_quantise(q):
+        def join(q):
+            e_grouped = qin.tile([P, UNIT, 4], BF16, tag="grouped", align_bytes=64)
+            nc.vector.scalar_tensor_tensor(
+                out=e_grouped[:],
+                in0=lin_tiles[q][:].rearrange("q t j -> q j t"),
+                scalar=neg_e0[:, q % 2 : q % 2 + 1],
+                in1=exp_tiles[q][:].rearrange("q t j -> q j t"),
+                op0=ALU.max,
+                op1=ALU.add,
+            )
+            grouped_tiles[q] = e_grouped
+
+        def quantise(q):
             u = q // 2
             c = q % 2
             if c == 0:
@@ -191,20 +213,10 @@ def tile_basicemotionpredictions_pa_t_kernel(tc, h2, gamma, beta, Wh, bh, out):
                 e_scales = codes.tile([P, PASSES, UNIT], U8, align_bytes=64)
                 code_tiles[u] = (e_codes, e_scales)
             e_codes, e_scales = code_tiles[u]
-            e_exp, e_lin = branch_tiles[q]
-            e_grouped = qin.tile([P, UNIT, 4], BF16, tag="grouped", align_bytes=64)
-            nc.vector.scalar_tensor_tensor(
-                out=e_grouped[:],
-                in0=e_lin[:].rearrange("q t j -> q j t"),
-                scalar=neg_e0[:],
-                in1=e_exp[:].rearrange("q t j -> q j t"),
-                op0=ALU.max,
-                op1=ALU.add,
-            )
             nc.vector.quantize_mx(
                 out=e_codes[:, c, :].bitcast(FP8X4),
                 scales=e_scales[:, c, :],
-                in_=e_grouped[:].rearrange("q j t -> q (j t)"),
+                in_=grouped_tiles[q][:].rearrange("q j t -> q (j t)"),
             )
 
         def products(i):
@@ -259,17 +271,26 @@ def tile_basicemotionpredictions_pa_t_kernel(tc, h2, gamma, beta, Wh, bh, out):
                 nc.scalar.activation(out=d_abs[:, nt, :], in_=d_t_tiles[i][nt][:], func=ACT.Abs)
             abs_tiles[i] = d_abs
 
-        def normalise_and_store(i):
+        def l1_sums(i):
             l1 = small.tile([P, 4, 512 // HEAD], F32)
-            r_l1 = small.tile([P, 4, 512 // HEAD], F32)
             nc.vector.tensor_reduce(
                 out=l1[:].rearrange("p nt g -> p (nt g)"),
                 in_=abs_tiles[i][:].rearrange("p nt (g e) -> p (nt g) e", e=HEAD),
                 axis=AXIS.X,
                 op=ALU.add,
             )
-            nc.vector.tensor_scalar_max(out=l1[:], in0=l1[:], scalar1=L1_EPS / SELU_SCALE)
-            nc.vector.reciprocal(out=r_l1[:], in_=l1[:])
+            l1_tiles[i] = l1
+
+        def l1_floor(i):
+            nc.vector.tensor_scalar_max(out=l1_tiles[i][:], in0=l1_tiles[i][:], scalar1=L1_EPS / SELU_SCALE)
+
+        def l1_reciprocal(i):
+            r_l1 = small.tile([P, 4, 512 // HEAD], F32)
+            nc.vector.reciprocal(out=r_l1[:], in_=l1_tiles[i][:])
+            l1_tiles[i] = r_l1
+
+        def normalise_and_store(i):
+            r_l1 = l1_tiles[i]
             out_sb = stream.tile([P, 4, 512], F32, tag="stream")
             for nt in range(4):
                 nc.vector.tensor_tensor(
@@ -282,23 +303,33 @@ def tile_basicemotionpredictions_pa_t_kernel(tc, h2, gamma, beta, Wh, bh, out):
             hf = i % 2
             nc.sync.dma_start(out=out_v[:, first_tile : first_tile + 4, 512 * hf : 512 * (hf + 1)], in_=out_sb[:])
 
+        def live(i):
+            return 0 <= i < steps
+
         with tc.manual_schedule():
             for i in range(-4, steps + 1):
-                if 0 <= i < steps:
+                if live(i):
                     head_branches(i)
-                if 0 <= i - 1 < steps:
+                if live(i - 1):
                     magnitudes(i - 1)
-                if 0 <= i + 4 < steps:
+                if live(i + 4):
                     linear_branch(i + 4)
-                if 0 <= i + 3 < steps:
+                if 0 <= i + 4 < 4:
+                    quantise_weights((i + 4) // 2, (i + 4) % 2)
+                if live(i + 2):
+                    join(i + 2)
+                if live(i + 3):
                     exp_branch(i + 3)
-                if 0 <= i + 2 < steps:
-                    join_and_quantise(i + 2)
-                if 0 <= i + 1 < steps:
+                if live(i + 2):
+                    quantise(i + 2)
+                if live(i + 1):
                     products(i + 1)
-                if 0 <= i < steps:
+                if live(i):
                     head_selu(i)
-                if 0 <= i - 1 < steps:
+                if live(i - 1):
+                    l1_sums(i - 1)
+                    l1_floor(i - 1)
+                    l1_reciprocal(i - 1)
                     normalise_and_store(i - 1)
-                if 0 <= i < steps:
+                if live(i):
                     transpose_back(i)

import math

import concourse.bass as bass
import concourse.mybir as mybir
import concourse.tile as tile
from concourse.masks import make_identity

F32 = mybir.dt.float32
BF16 = mybir.dt.bfloat16
U32 = mybir.dt.uint32
U8 = mybir.dt.uint8
FP8X4 = mybir.dt.float8_e4m3fn_x4
ALU = mybir.AluOpType
ACT = mybir.ActivationFunctionType
AXIS = mybir.AxisListType

P = 128
ROWS = 4096
HID = 1024
OUTS = 1024
HEAD = 32
ROW_TILES = ROWS // P
WORD_BLOCKS = HID // 2 // P
PLANES = 2 * WORD_BLOCKS
PASSES = HID // 512

LOAD_TILES = 4
LOAD_COLS = LOAD_TILES * P
STAT_COLS = 256
UNIT = 512

BN_EPS = 1e-5
L1_EPS = 1e-12
SELU_ALPHA = 1.6732632423543772
SELU_SCALE = 1.0507009873554805
SA = SELU_SCALE * SELU_ALPHA

FLOPS = 2 * ROWS * HID * OUTS


def tile_basicemotionpredictions_pa_t_kernel(tc, h2, gamma, beta, Wh, bh, out):
    nc = tc.nc
    h2_v = h2.rearrange("(p n) f -> p n f", n=ROW_TILES)
    out_v = out.rearrange("(p n) h g e -> p n (h g e)", n=ROW_TILES)
    wh_v = Wh.rearrange("h g (cu q e2) e -> q (h g cu) (e2 e)", cu=WORD_BLOCKS, q=P, e2=2)

    with tc.tile_pool(name="keep", bufs=1) as keep, tc.tile_pool(name="stream", bufs=3) as stream, tc.tile_pool(
        name="qin", bufs=2
    ) as qin, tc.tile_pool(name="work", bufs=3) as work, tc.tile_pool(name="codes", bufs=4) as codes, tc.tile_pool(
        name="post", bufs=2
    ) as post, tc.tile_pool(name="small", bufs=3) as small, tc.psum_pool(name="psum_mm", bufs=4) as psum_mm, tc.psum_pool(
        name="psum_tr", bufs=4
    ) as psum_tr:
        warm = keep.tile([P, 1], F32)
        nc.vector.memset(warm[:], 1.0)
        warm_out = keep.tile([P, 1], F32)
        nc.scalar.activation(out=warm_out[:], in_=warm[:], func=ACT.Sqrt)
        zero = keep.tile([P, 1], F32)
        nc.vector.memset(zero[:], 0.0)
        minus_sa = keep.tile([P, 1], F32)
        nc.vector.tensor_scalar_add(out=minus_sa[:], in0=zero[:], scalar1=-SA)
        exp_bias = keep.tile([P, 1], F32)
        nc.vector.tensor_scalar_add(out=exp_bias[:], in0=zero[:], scalar1=SELU_ALPHA + math.log(SA))
        ln_sa = keep.tile([P, 1], F32)
        nc.vector.tensor_scalar_add(out=ln_sa[:], in0=zero[:], scalar1=math.log(SA))

        ident = keep.tile([P, P], F32)
        make_identity(nc, ident[:])

        gamma_sb = keep.tile([P, WORD_BLOCKS, 2], BF16)
        beta_sb = keep.tile([P, WORD_BLOCKS, 2], BF16)
        bh_sb = keep.tile([P, OUTS // P], BF16)
        nc.scalar.dma_start(out=gamma_sb[:], in_=gamma.rearrange("(wb q e2) -> q wb e2", wb=WORD_BLOCKS, q=P))
        nc.scalar.dma_start(out=beta_sb[:], in_=beta.rearrange("(wb q e2) -> q wb e2", wb=WORD_BLOCKS, q=P))
        with nc.allow_non_contiguous_dma(reason="1,024 bias values, one output to a partition"):
            nc.scalar.dma_start(out=bh_sb[:], in_=bh.rearrange("h g e -> (h g e)").rearrange("(ob o) -> o ob", o=P))

        bias_rel = keep.tile([P, OUTS // P], F32)
        bias_exp = keep.tile([P, OUTS // P], F32)
        nc.vector.tensor_copy(out=bias_rel[:], in_=bh_sb[:])
        nc.vector.tensor_scalar_add(out=bias_exp[:], in0=bias_rel[:], scalar1=math.log(SELU_ALPHA))

        x_t = keep.tile([P, WORD_BLOCKS, ROWS], F32)
        stats = keep.tile([P, WORD_BLOCKS, ROWS // STAT_COLS, 6], F32)
        for ld in range(ROW_TILES // LOAD_TILES):
            x_sb = stream.tile([P, LOAD_TILES, HID], BF16, tag="stream")
            nc.sync.dma_start(out=x_sb[:], in_=h2_v[:, LOAD_TILES * ld : LOAD_TILES * (ld + 1), :])
            for wb in range(WORD_BLOCKS):
                xt_ps = psum_tr.tile([P, LOAD_COLS], F32, tag="tr")
                for i in range(LOAD_TILES):
                    nc.tensor.transpose(
                        xt_ps[:, P * i : P * (i + 1)],
                        x_sb[:, i, :].bitcast(F32)[:, P * wb : P * (wb + 1)],
                        ident[:],
                    )
                nc.scalar.copy(out=x_t[:, wb, LOAD_COLS * ld : LOAD_COLS * (ld + 1)], in_=xt_ps[:])
                for s in range(LOAD_COLS // STAT_COLS):
                    first = LOAD_COLS * ld + STAT_COLS * s
                    nc.vector.bn_stats(
                        out=stats[:, wb, first // STAT_COLS, :],
                        in_=x_t[:, wb, first : first + STAT_COLS].bitcast(BF16),
                    )

        w_raws = []
        for hf in range(2):
            w_raw = stream.tile([P, 16, PLANES, HEAD], BF16, tag="stream")
            nc.sync.dma_start(
                out=w_raw[:].rearrange("q hg (cu e2) e -> q (hg cu) (e2 e)", e2=2),
                in_=wh_v[:, 64 * hf : 64 * (hf + 1), :],
            )
            w_raws.append(w_raw)

        mv = keep.tile([P, PLANES, 2], F32)
        for wb in range(WORD_BLOCKS):
            for e2 in range(2):
                nc.vector.bn_aggr(out=mv[:, 2 * wb + e2, :], in_=stats[:, wb, :, 3 * e2 : 3 * e2 + 3])
        var_eps = keep.tile([P, PLANES], F32)
        std = keep.tile([P, PLANES], F32)
        rstd = keep.tile([P, PLANES], F32)
        a_lin = keep.tile([P, PLANES], F32)
        b_neg = keep.tile([P, PLANES], F32)
        a_rel = keep.tile([P, PLANES], F32)
        b_rel = keep.tile([P, PLANES], F32)
        nc.vector.tensor_scalar_add(out=var_eps[:], in0=mv[:, :, 1], scalar1=BN_EPS)
        nc.scalar.activation(out=std[:], in_=var_eps[:], func=ACT.Sqrt)
        nc.vector.reciprocal(out=rstd[:], in_=std[:])
        nc.vector.tensor_tensor(out=a_lin[:], in0=gamma_sb[:].rearrange("q wb e2 -> q (wb e2)"), in1=rstd[:], op=ALU.mult)
        nc.vector.tensor_tensor(out=b_neg[:], in0=mv[:, :, 0], in1=a_lin[:], op=ALU.mult)
        nc.vector.tensor_tensor(out=b_neg[:], in0=b_neg[:], in1=beta_sb[:].rearrange("q wb e2 -> q (wb e2)"), op=ALU.subtract)
        nc.vector.tensor_scalar_mul(out=a_rel[:], in0=a_lin[:], scalar1=SELU_SCALE)
        neg_e0 = keep.tile([P, PASSES], F32)
        nc.scalar.activation(out=neg_e0[:, 0:1], in_=zero[:], func=ACT.Exp, scale=-1.0 / SELU_SCALE, bias=ln_sa[:])
        nc.scalar.activation(out=neg_e0[:, 1:2], in_=minus_sa[:], func=ACT.Exp, scale=1.0 / SELU_SCALE, bias=exp_bias[:])
        nc.vector.tensor_scalar_mul(out=neg_e0[:], in0=neg_e0[:], scalar1=-1.0)
        for c in range(PASSES):
            nc.vector.tensor_scalar(
                out=b_rel[:, 4 * c : 4 * (c + 1)], in0=b_neg[:, 4 * c : 4 * (c + 1)],
                scalar1=-SELU_SCALE, scalar2=neg_e0[:, c : c + 1], op0=ALU.mult, op1=ALU.add,
            )

        w_codes = keep.tile([P, 2, PASSES, 512], U32, align_bytes=64)
        w_scales = keep.tile([P, 2, PASSES, 512], U8, align_bytes=64)

        def quantise_weights(hf, c):
            w_grouped = qin.tile([P, 512, 4], BF16, tag="grouped", align_bytes=64)
            nc.vector.tensor_copy(
                out=w_grouped[:].rearrange("q (hg e) t -> q hg e t", e=HEAD),
                in_=w_raws[hf][:, :, 4 * c : 4 * (c + 1), :].rearrange("q hg t e -> q hg e t"),
            )
            nc.vector.quantize_mx(
                out=w_codes[:, hf, c, :].bitcast(FP8X4),
                scales=w_scales[:, hf, c, :],
                in_=w_grouped[:].rearrange("q o t -> q (o t)"),
            )

        steps = 2 * (ROWS // UNIT)
        lin_tiles = {}
        exp_tiles = {}
        grouped_tiles = {}
        code_tiles = {}
        acc_tiles = {}
        z_tiles = {}
        d_t_tiles = {}
        abs_tiles = {}
        l1_tiles = {}

        def linear_branch(q):
            u = q // 2
            c = q % 2
            e_lin = work.tile([P, 4, UNIT], F32, bufs=3)
            for t in range(4):
                wb = 2 * c + t // 2
                plane = 4 * c + t
                x_plane = (
                    x_t[:, wb, UNIT * u : UNIT * (u + 1)]
                    .bitcast(BF16)
                    .rearrange("q (j e2) -> q j e2", e2=2)[:, :, t % 2]
                )
                nc.gpsimd.tensor_scalar(
                    out=e_lin[:, t, :], in0=x_plane,
                    scalar1=a_rel[:, plane : plane + 1], scalar2=b_rel[:, plane : plane + 1],
                    op0=ALU.mult, op1=ALU.add,
                )
            lin_tiles[q] = e_lin

        def exp_branch(q):
            e_exp = work.tile([P, 4, UNIT], F32, bufs=2)
            if q % 2 == 0:
                nc.scalar.activation(out=e_exp[:], in_=lin_tiles[q][:], func=ACT.Relu, scale=-1.0, bias=minus_sa[:])
                nc.scalar.activation(out=e_exp[:], in_=e_exp[:], func=ACT.Exp, scale=-1.0 / SELU_SCALE, bias=ln_sa[:])
            else:
                nc.vector.tensor_scalar_min(out=e_exp[:], in0=lin_tiles[q][:], scalar1=-SA)
                nc.scalar.activation(out=e_exp[:], in_=e_exp[:], func=ACT.Exp, scale=1.0 / SELU_SCALE, bias=exp_bias[:])
            exp_tiles[q] = e_exp

        def join(q):
            e_grouped = qin.tile([P, UNIT, 4], BF16, tag="grouped", align_bytes=64)
            nc.vector.scalar_tensor_tensor(
                out=e_grouped[:],
                in0=lin_tiles[q][:].rearrange("q t j -> q j t"),
                scalar=neg_e0[:, q % 2 : q % 2 + 1],
                in1=exp_tiles[q][:].rearrange("q t j -> q j t"),
                op0=ALU.max,
                op1=ALU.add,
            )
            grouped_tiles[q] = e_grouped

        def quantise(q):
            u = q // 2
            c = q % 2
            if c == 0:
                e_codes = codes.tile([P, PASSES, UNIT], U32, align_bytes=64)
                e_scales = codes.tile([P, PASSES, UNIT], U8, align_bytes=64)
                code_tiles[u] = (e_codes, e_scales)
            e_codes, e_scales = code_tiles[u]
            nc.vector.quantize_mx(
                out=e_codes[:, c, :].bitcast(FP8X4),
                scales=e_scales[:, c, :],
                in_=grouped_tiles[q][:].rearrange("q j t -> q (j t)"),
            )

        def products(i):
            hf = i % 2
            e_codes, e_scales = code_tiles[i // 2]
            accs = []
            for ob4 in range(4):
                w_cols = slice(P * ob4, P * (ob4 + 1))
                acc = psum_mm.tile([P, UNIT], F32)
                for c in range(PASSES):
                    nc.tensor.matmul_mx(
                        out=acc[:],
                        lhsT=w_codes[:, hf, c, w_cols].bitcast(FP8X4),
                        lhsT_scale=w_scales[:, hf, c, w_cols],
                        rhs=e_codes[:, c, :].bitcast(FP8X4),
                        rhs_scale=e_scales[:, c, :],
                        start=(c == 0),
                        stop=(c == PASSES - 1),
                    )
                accs.append(acc)
            acc_tiles[i] = accs

        def head_branches(i):
            z_exp = post.tile([P, 4, UNIT], F32)
            z_rel = post.tile([P, 4, UNIT], F32)
            for ob4 in range(4):
                ob = 4 * (i % 2) + ob4
                acc = acc_tiles[i][ob4]
                nc.scalar.activation(out=z_exp[:, ob4, :], in_=acc[:], func=ACT.Exp, bias=bias_exp[:, ob : ob + 1])
                nc.scalar.activation(out=z_rel[:, ob4, :], in_=acc[:], func=ACT.Relu, bias=bias_rel[:, ob : ob + 1])
            z_tiles[i] = (z_exp, z_rel)

        def head_selu(i):
            z_exp, z_rel = z_tiles[i]
            nc.vector.scalar_tensor_tensor(
                out=z_exp[:], in0=z_exp[:], scalar=-SELU_ALPHA, in1=z_rel[:], op0=ALU.add, op1=ALU.min
            )

        def transpose_back(i):
            z_exp = z_tiles[i][0]
            d_ts = []
            for nt in range(4):
                d_t = psum_tr.tile([P, 512], F32, tag="tr")
                for ob4 in range(4):
                    nc.tensor.transpose(d_t[:, P * ob4 : P * (ob4 + 1)], z_exp[:, ob4, P * nt : P * (nt + 1)], ident[:])
                d_ts.append(d_t)
            d_t_tiles[i] = d_ts

        def magnitudes(i):
            d_abs = post.tile([P, 4, 512], F32)
            for nt in range(4):
                nc.scalar.activation(out=d_abs[:, nt, :], in_=d_t_tiles[i][nt][:], func=ACT.Abs)
            abs_tiles[i] = d_abs

        def l1_sums(i):
            l1 = small.tile([P, 4, 512 // HEAD], F32)
            nc.vector.tensor_reduce(
                out=l1[:].rearrange("p nt g -> p (nt g)"),
                in_=abs_tiles[i][:].rearrange("p nt (g e) -> p (nt g) e", e=HEAD),
                axis=AXIS.X,
                op=ALU.add,
            )
            l1_tiles[i] = l1

        def l1_floor(i):
            nc.vector.tensor_scalar_max(out=l1_tiles[i][:], in0=l1_tiles[i][:], scalar1=L1_EPS / SELU_SCALE)

        def l1_reciprocal(i):
            r_l1 = small.tile([P, 4, 512 // HEAD], F32)
            nc.vector.reciprocal(out=r_l1[:], in_=l1_tiles[i][:])
            l1_tiles[i] = r_l1

        def normalise_and_store(i):
            r_l1 = l1_tiles[i]
            out_sb = stream.tile([P, 4, 512], F32, tag="stream")
            for nt in range(4):
                nc.vector.tensor_tensor(
                    out=out_sb[:, nt, :].rearrange("p (g e) -> p g e", e=HEAD),
                    in0=d_t_tiles[i][nt][:].rearrange("p (g e) -> p g e", e=HEAD),
                    in1=r_l1[:, nt, :].unsqueeze(2).to_broadcast([P, 512 // HEAD, HEAD]),
                    op=ALU.mult,
                )
            first_tile = UNIT * (i // 2) // P
            hf = i % 2
            nc.sync.dma_start(out=out_v[:, first_tile : first_tile + 4, 512 * hf : 512 * (hf + 1)], in_=out_sb[:])

        def live(i):
            return 0 <= i < steps

        with tc.manual_schedule():
            for i in range(-4, steps + 1):
                if live(i):
                    head_branches(i)
                if live(i - 1):
                    magnitudes(i - 1)
                if live(i + 4):
                    linear_branch(i + 4)
                if 0 <= i + 4 < 4:
                    quantise_weights((i + 4) // 2, (i + 4) % 2)
                if live(i + 2):
                    join(i + 2)
                if live(i + 3):
                    exp_branch(i + 3)
                if live(i + 2):
                    quantise(i + 2)
                if live(i + 1):
                    products(i + 1)
                if live(i):
                    head_selu(i)
                if live(i - 1):
                    l1_sums(i - 1)
                    l1_floor(i - 1)
                    l1_reciprocal(i - 1)
                    normalise_and_store(i - 1)
                if live(i):
                    transpose_back(i)
